import numpy as np
import ml_dtypes


def mxq(x, axis, fmt="e4m3"):
    dtype, down = {"e4m3": (ml_dtypes.float8_e4m3fn, 7), "e5m2": (ml_dtypes.float8_e5m2, 14)}[fmt]
    v = np.moveaxis(np.asarray(x, np.float32).astype(ml_dtypes.bfloat16).astype(np.float64), axis, -1)
    blocks = v.reshape(v.shape[:-1] + (-1, 32))
    amax = np.abs(blocks).max(-1, keepdims=True)
    byte = np.maximum(np.where(amax > 0, np.frexp(amax)[1] - 1 + 127, 0) - down, 1)
    scale = np.exp2(byte - 127.0)
    codes = (blocks / scale).astype(np.float32).astype(dtype).astype(np.float64)
    return np.moveaxis((codes * scale).reshape(v.shape), -1, axis)


WIDE = False


def mx_kscale(k):
    if not WIDE:
        return np.ones(k)
    levels = np.array([10, -10, 5, -5, 0])
    if k % 512:
        return np.exp2(np.random.permutation(np.resize(levels, k // 32))).repeat(32)
    a = np.empty((k // 512, 16))
    for p in range(k // 512):
        a[p, :8] = np.random.permutation(np.resize(levels, 8))
        for g in range(8):
            far = levels[np.abs(levels - a[p, g]) >= 10]
            a[p, g + 8] = far[np.random.randint(len(far))]
    return np.exp2(a.ravel()).repeat(32)


BF16 = ml_dtypes.bfloat16


def bf(x):
    return np.asarray(x, np.float32).astype(BF16)


def f64(x):
    return np.asarray(x).astype(np.float64)


B, S, H, D = 2, 256, 12, 128
DIM = H * D
EPS = 1e-6
QK_RMS = 0.004


def rmsnorm(x, w):
    var = np.mean(x * x, axis=-1, keepdims=True)
    return x * (1.0 / np.sqrt(var + EPS)) * w


def apply_rope(x, freqs_cis):
    x_ = x.reshape(B, H, S, D // 2, 1, 2)
    out = freqs_cis[..., 0] * x_[..., 0] + freqs_cis[..., 1] * x_[..., 1]
    return out.reshape(B, H, S, D)


def heads(t):
    return t.reshape(B, S, H, D).transpose(0, 2, 1, 3)


def draw0():
    s = mx_kscale(DIM)
    col = np.repeat(np.array([QK_RMS, QK_RMS, 1.0]), DIM)
    return {"hidden_states": bf(np.random.standard_normal((B, S, DIM)) * s),
            "image_rotary_emb": bf(np.random.standard_normal((1, 1, S, D // 2, 2, 2))),
            "w_qkv": bf(np.random.standard_normal((DIM, 3 * DIM)) * col / np.sqrt(DIM) / s[:, None]),
            "b_qkv": bf(np.random.standard_normal(3 * DIM) * 0.5 * col),
            "norm_q_w": bf(1.0 + 0.1 * np.random.standard_normal(D)),
            "norm_k_w": bf(1.0 + 0.1 * np.random.standard_normal(D))}


def core(hidden_states, image_rotary_emb, w_qkv, b_qkv, norm_q_w, norm_k_w):
    xq = mxq(f64(hidden_states), 2, "e4m3")
    w = f64(w_qkv).reshape(DIM, 3, DIM)
    b = f64(b_qkv).reshape(3, DIM)
    f = f64(image_rotary_emb)
    q = heads((xq @ mxq(w[:, 0], 0, "e4m3")) + b[0])
    k = heads((xq @ mxq(w[:, 1], 0, "e4m3")) + b[1])
    v = heads((xq @ mxq(w[:, 2], 0, "e4m3")) + b[2])
    q = apply_rope(rmsnorm(q, f64(norm_q_w)), f)
    k = apply_rope(rmsnorm(k, f64(norm_k_w)), f)
    return q, k, v


def e4m3fn_bytes(y):
    return np.clip(np.asarray(y, np.float64), -448.0, 448.0).astype(np.float32).astype(ml_dtypes.float8_e4m3fn).view(np.uint8)


def e4m3fn_values(b):
    return np.asarray(b, np.uint8).view(ml_dtypes.float8_e4m3fn).astype(np.float64)


def setup_inputs():
    d = draw0()
    x0 = np.asarray(d['w_qkv']).astype(np.float64)
    s = (np.max(np.abs(x0), axis=(1,), keepdims=True) / 448.0).astype(np.float32)
    out = {}
    for k, v in d.items():
        if k == 'w_qkv':
            out['w_qkv_bytes'] = e4m3fn_bytes(x0 / s.astype(np.float64))
            out['w_qkv_scale'] = s
        else:
            out[k] = v
    return out


def reference(hidden_states, image_rotary_emb, w_qkv_bytes, w_qkv_scale, b_qkv, norm_q_w, norm_k_w):
    return core(hidden_states, image_rotary_emb, e4m3fn_values(w_qkv_bytes) * w_qkv_scale.astype(np.float64), b_qkv, norm_q_w, norm_k_w)

@@ -1,0 +1,273 @@
+from contextlib import ExitStack
+
+import concourse.mybir as mybir
+from concourse.masks import make_identity
+
+B, S, H, D = 2, 256, 12, 128
+DIM = H * D
+TOK = B * S
+EPS = 1e-6
+
+FLOPS = 2 * TOK * DIM * 3 * DIM
+
+F32 = mybir.dt.float32
+BF16 = mybir.dt.bfloat16
+U32 = mybir.dt.uint32
+U8 = mybir.dt.uint8
+FP8 = mybir.dt.float8_e4m3fn
+FP8X4 = mybir.dt.float8_e4m3fn_x4
+ACT = mybir.ActivationFunctionType
+ALU = mybir.AluOpType
+
+P = 128
+PACK = 4
+K_PASS = P * PACK
+PASSES = DIM // K_PASS
+CW = 512
+HEADS_PER_CHUNK = CW // D
+TOK_TILES = TOK // P
+CHUNK_ORDER = (0, 3, 6, 1, 4, 7, 2, 5, 8)
+
+
+def widen_on_vector(n, t):
+    if n < PASSES:
+        return t >= 2
+    return n % 5 == 4 and t == 3
+
+
+def tile_fluxsingleattention_pa_kernel(
+    tc, hidden_states, image_rotary_emb, w_qkv_bytes, w_qkv_scale, b_qkv, norm_q_w, norm_k_w, out_0, out_1, out_2
+):
+    nc = tc.nc
+    with ExitStack() as ctx:
+        const = ctx.enter_context(tc.tile_pool(name="const", bufs=1))
+        wload = ctx.enter_context(tc.tile_pool(name="wload", bufs=len(CHUNK_ORDER) * PASSES))
+        prep = ctx.enter_context(tc.tile_pool(name="prep", bufs=3))
+        epi = ctx.enter_context(tc.tile_pool(name="epi", bufs=3))
+        psum = ctx.enter_context(tc.psum_pool(name="psum", bufs=2))
+
+        one_col = const.tile([P, 2], F32, name="one_col")
+        nc.vector.memset(one_col[:], 1.0)
+        warm = const.tile([P, 1], F32, name="warm")
+        nc.scalar.activation(out=warm[:], in_=one_col[:, 0:1], func=ACT.Sqrt)
+        ident = const.tile([P, P], F32, name="ident")
+        make_identity(nc, ident[:])
+        ident_bf = const.tile([P, P], BF16, name="ident_bf")
+        make_identity(nc, ident_bf[:])
+        swap = const.tile([P, P], F32, name="swap")
+        ident_pairs = ident[:].rearrange("p (q j) -> p q j", j=2)
+        swap_pairs = swap[:].rearrange("p (q j) -> p q j", j=2)
+        nc.vector.tensor_copy(out=swap_pairs[:, :, 0], in_=ident_pairs[:, :, 1])
+        nc.vector.tensor_copy(out=swap_pairs[:, :, 1], in_=ident_pairs[:, :, 0])
+        stage = const.tile([P, P], BF16, name="stage")
+        nc.vector.memset(stage[:], 0.0)
+
+        x_rows = hidden_states.flatten_outer_dims().rearrange("(i p) k -> i p k", p=P)
+        w_rows = w_qkv_bytes.rearrange("(g p t) n -> g p t n", p=P, t=PACK)
+        units = [(c, g) for c in CHUNK_ORDER for g in range(PASSES)]
+
+        wscale = const.tile([P, PASSES, PACK], F32, name="wscale")
+        nc.sync.dma_start(out=wscale[:], in_=w_qkv_scale.rearrange("(g p t) o -> p g (t o)", p=P, t=PACK))
+
+        wbytes = {}
+
+        def load_unit(n):
+            c, g = units[n]
+            wb = wload.tile([P, PACK, CW], U8, name="wbytes")
+            nc.sync.dma_start(out=wb[:], in_=w_rows[g][:, :, c * CW : (c + 1) * CW])
+            wbytes[n] = wb
+
+        x_sb = []
+
+        def load_x(i):
+            xs = const.tile([P, DIM], BF16, name="x_sb%d" % i)
+            nc.sync.dma_start(out=xs[:], in_=x_rows[i])
+            x_sb.append(xs)
+
+        load_unit(0)
+        load_x(0)
+        load_x(1)
+        load_unit(1)
+        load_x(2)
+        load_x(3)
+        load_unit(2)
+        nc.sync.dma_start(out=stage[0:36, :], in_=b_qkv.rearrange("(r d) -> r d", d=D))
+        nc.sync.dma_start(out=stage[36:37, :], in_=norm_q_w.rearrange("(o d) -> o d", o=1))
+        nc.sync.dma_start(out=stage[37:38, :], in_=norm_k_w.rearrange("(o d) -> o d", o=1))
+        f_sb = const.tile([P, 2, 2 * D], BF16, name="f_sb")
+        nc.sync.dma_start(out=f_sb[:], in_=image_rotary_emb.rearrange("o n (a s) q i j -> s (o n a) (q i j)", s=P))
+        for n in range(3, len(units)):
+            load_unit(n)
+        bias_v = const.tile([P, DIM], BF16, name="bias_v")
+        nc.sync.dma_start(out=bias_v[:], in_=b_qkv[2 * DIM : 3 * DIM].partition_broadcast(P))
+
+        x_codes = const.tile([P, PASSES, TOK], U32, name="x_codes", align_bytes=64)
+        x_scl = const.tile([P, PASSES, TOK], U8, name="x_scl", align_bytes=64)
+        for g in range(PASSES):
+            xg = const.tile([P, TOK * PACK], BF16, name="xg%d" % g, align_bytes=64)
+            xg_words = xg[:].bitcast(F32).rearrange("p (r u) -> p r u", u=2)
+            for hf in range(2):
+                xt = psum.tile([P, 2, 2 * P], F32, name="acc", bufs=3)
+                for i2 in range(2):
+                    words = x_sb[2 * hf + i2][:].bitcast(F32)
+                    for u in range(2):
+                        nc.tensor.transpose(
+                            xt[:, u, i2 * P : (i2 + 1) * P], words[:, 256 * g + u : 256 * (g + 1) : 2], ident[:]
+                        )
+                nc.vector.tensor_copy(
+                    out=xg_words[:, 2 * P * hf : 2 * P * (hf + 1), :], in_=xt[:].rearrange("p u r -> p r u")
+                )
+            nc.vector.quantize_mx(out=x_codes[:, g, :].bitcast(FP8X4), scales=x_scl[:, g, :], in_=xg[:])
+
+        cols_ps = psum.tile([P, P], BF16, name="setup", bufs=1)
+        nc.tensor.transpose(cols_ps[:], stage[:], ident_bf[:])
+        cols = const.tile([P, 38], F32, name="cols")
+        nc.vector.tensor_copy(out=cols[:], in_=cols_ps[:, 0:38])
+
+        f4 = f_sb[:].rearrange("p a (q e) -> p a q e", e=4)
+        f_same = const.tile([P, 2, D // 2, 2], F32, name="f_same")
+        f_cross = const.tile([P, 2, D // 2, 2], F32, name="f_cross")
+        for j in range(2):
+            nc.vector.tensor_copy(out=f_same[:, :, :, j], in_=f4[:, :, :, 3 * j])
+            nc.vector.tensor_copy(out=f_cross[:, :, :, j], in_=f4[:, :, :, 2 - j])
+        g_ps = psum.tile([P, 4, P], F32, name="rot", bufs=2)
+        for kind, src in enumerate((f_same, f_cross)):
+            for a in range(2):
+                nc.tensor.transpose(g_ps[:, 2 * kind + a, :], src[:, a].rearrange("p q j -> p (q j)"), ident[:])
+        rope = []
+        for qk in range(2):
+            pair = []
+            for kind in range(2):
+                gt = const.tile([P, TOK], F32, name="rope%d%d" % (qk, kind))
+                for b in range(B):
+                    nc.vector.tensor_scalar(
+                        out=gt[:, b * S : (b + 1) * S],
+                        in0=g_ps[:, 2 * kind : 2 * kind + 2, :].rearrange("p a s -> p (a s)"),
+                        scalar1=cols[:, 36 + qk : 37 + qk],
+                        scalar2=None,
+                        op0=ALU.mult,
+                    )
+                pair.append(gt)
+            rope.append(pair)
+
+        planes = {}
+        grouped = {}
+        w_codes = {}
+        w_scl = {}
+
+        def widen(n):
+            c, g = units[n]
+            pl = prep.tile([P, PACK, CW], BF16, name="planes", bufs=6)
+            for t in range(PACK):
+                src = wbytes[n][:, t, :].bitcast(FP8)
+                if widen_on_vector(n, t):
+                    nc.vector.tensor_scalar(
+                        out=pl[:, t, :], in0=src, scalar1=wscale[:, g, t : t + 1], scalar2=None, op0=ALU.mult
+                    )
+                else:
+                    nc.scalar.activation(out=pl[:, t, :], in_=src, func=ACT.Copy, scale=wscale[:, g, t : t + 1])
+            planes[n] = pl
+
+        def interleave(n):
+            gr = prep.tile([P, CW, PACK], BF16, name="grouped", bufs=3, align_bytes=64)
+            nc.vector.tensor_copy(out=gr[:], in_=planes[n][:].rearrange("p t c -> p c t"))
+            grouped[n] = gr
+
+        def quantise(n):
+            c, g = units[n]
+            if g == 0:
+                wc = prep.tile([P, PASSES, CW], U32, name="w_codes", bufs=4, align_bytes=64)
+                ws = prep.tile([P, PASSES, CW], U8, name="w_scl", bufs=4, align_bytes=64)
+                w_codes[c] = wc
+                w_scl[c] = ws
+            nc.vector.quantize_mx(
+                out=w_codes[c][:, g, :].bitcast(FP8X4),
+                scales=w_scl[c][:, g, :],
+                in_=grouped[n][:].rearrange("p c t -> p (c t)"),
+            )
+
+        def head(c, j):
+            qk = c // 3
+            h = (c % 3) * HEADS_PER_CHUNK + j
+            bcol = cols[:, qk * H + h : qk * H + h + 1]
+            dst = out_0 if qk == 0 else out_1
+            cs = slice(j * D, (j + 1) * D)
+            acc = psum.tile([P, TOK], F32, name="acc", bufs=3)
+            for g in range(PASSES):
+                nc.tensor.matmul_mx(
+                    out=acc[:],
+                    lhsT=w_codes[c][:, g, cs].bitcast(FP8X4),
+                    lhsT_scale=w_scl[c][:, g, cs],
+                    rhs=x_codes[:, g, :].bitcast(FP8X4),
+                    rhs_scale=x_scl[:, g, :],
+                    start=(g == 0),
+                    stop=(g == PASSES - 1),
+                )
+            same = epi.tile([P, TOK], F32, name="same")
+            cross = epi.tile([P, TOK], F32, name="cross")
+            sq = epi.tile([P, TOK], F32, name="sq")
+            nc.vector.scalar_tensor_tensor(
+                out=same[:], in0=acc[:], scalar=bcol, in1=rope[qk][0][:], op0=ALU.add, op1=ALU.mult
+            )
+            nc.vector.scalar_tensor_tensor(
+                out=cross[:], in0=acc[:], scalar=bcol, in1=rope[qk][1][:], op0=ALU.add, op1=ALU.mult
+            )
+            nc.scalar.activation(out=sq[:], in_=acc[:], func=ACT.Square, bias=bcol, scale=1.0)
+            rot = psum.tile([P, TOK_TILES, D], F32, name="rot", bufs=2)
+            ssq = psum.tile([P, TOK_TILES, 2], F32, name="ssq", bufs=2)
+            for i in range(TOK_TILES):
+                ts = slice(i * P, (i + 1) * P)
+                nc.tensor.matmul(out=rot[:, i, :], lhsT=same[:, ts], rhs=ident[:], is_transpose=True, start=True, stop=False)
+                nc.tensor.matmul(out=rot[:, i, :], lhsT=cross[:, ts], rhs=swap[:], is_transpose=True, start=False, stop=True)
+            for i in range(TOK_TILES):
+                ts = slice(i * P, (i + 1) * P)
+                nc.tensor.matmul(out=ssq[:, i, :], lhsT=sq[:, ts], rhs=one_col[:], start=True, stop=True)
+            rms = epi.tile([P, TOK_TILES], F32, name="rms")
+            rstd = epi.tile([P, TOK_TILES], F32, name="rstd")
+            nc.scalar.activation(out=rms[:], in_=ssq[:, :, 0], func=ACT.Sqrt, bias=EPS, scale=1.0 / D)
+            nc.vector.reciprocal(out=rstd[:], in_=rms[:])
+            res = epi.tile([P, TOK_TILES, D], F32, name="res", bufs=6)
+            for i in range(TOK_TILES):
+                nc.scalar.activation(out=res[:, i, :], in_=rot[:, i, :], func=ACT.Copy, scale=rstd[:, i : i + 1])
+            for b in range(B):
+                nc.sync.dma_start(out=dst[b, h].rearrange("(a s) d -> s a d", s=P), in_=res[:, 2 * b : 2 * b + 2, :])
+
+        def value_tile(c, i):
+            h0 = (c - 6) * HEADS_PER_CHUNK
+            ts = slice(i * P, (i + 1) * P)
+            acc = psum.tile([P, CW], F32, name="acc", bufs=3)
+            for g in range(PASSES):
+                nc.tensor.matmul_mx(
+                    out=acc[:],
+                    lhsT=x_codes[:, g, ts].bitcast(FP8X4),
+                    lhsT_scale=x_scl[:, g, ts],
+                    rhs=w_codes[c][:, g, :].bitcast(FP8X4),
+                    rhs_scale=w_scl[c][:, g, :],
+                    start=(g == 0),
+                    stop=(g == PASSES - 1),
+                )
+            val = epi.tile([P, CW], F32, name="val", bufs=4)
+            nc.vector.tensor_tensor(out=val[:], in0=acc[:], in1=bias_v[:, (c - 6) * CW : (c - 5) * CW], op=ALU.add)
+            b, a = divmod(i, 2)
+            nc.sync.dma_start(
+                out=out_2[b, h0 : h0 + HEADS_PER_CHUNK, a * P : (a + 1) * P, :].rearrange("h s d -> s h d"),
+                in_=val[:].rearrange("p (h d) -> p h d", d=D),
+            )
+
+        def finish_chunk(c):
+            if c < 6:
+                for j in range(HEADS_PER_CHUNK):
+                    head(c, j)
+            else:
+                for i in range(TOK_TILES):
+                    value_tile(c, i)
+
+        for n in range(len(units) + 1):
+            if n < len(units):
+                widen(n)
+                interleave(n)
+            if n >= 1:
+                quantise(n - 1)
+                c, g = units[n - 1]
+                if g == PASSES - 1:
+                    finish_chunk(c)

@@ -24,6 +24,7 @@ PACK = 4
 K_PASS = P * PACK
 PASSES = DIM // K_PASS
 CW = 512
+SSN = 128
 HEADS_PER_CHUNK = CW // D
 TOK_TILES = TOK // P
 CHUNK_ORDER = (0, 3, 6, 1, 4, 7, 2, 5, 8)
@@ -46,7 +47,7 @@ def tile_fluxsingleattention_pa_kernel(
         epi = ctx.enter_context(tc.tile_pool(name="epi", bufs=3))
         psum = ctx.enter_context(tc.psum_pool(name="psum", bufs=2))
 
-        one_col = const.tile([P, 2], F32, name="one_col")
+        one_col = const.tile([P, SSN], F32, name="one_col")
         nc.vector.memset(one_col[:], 1.0)
         warm = const.tile([P, 1], F32, name="warm")
         nc.scalar.activation(out=warm[:], in_=one_col[:, 0:1], func=ACT.Sqrt)
@@ -214,7 +215,7 @@ def tile_fluxsingleattention_pa_kernel(
             )
             nc.scalar.activation(out=sq[:], in_=acc[:], func=ACT.Square, bias=bcol, scale=1.0)
             rot = psum.tile([P, TOK_TILES, D], F32, name="rot", bufs=2)
-            ssq = psum.tile([P, TOK_TILES, 2], F32, name="ssq", bufs=2)
+            ssq = psum.tile([P, TOK_TILES, SSN], F32, name="ssq", bufs=2)
             for i in range(TOK_TILES):
                 ts = slice(i * P, (i + 1) * P)
                 nc.tensor.matmul(out=rot[:, i, :], lhsT=same[:, ts], rhs=ident[:], is_transpose=True, start=True, stop=False)

@@ -24,16 +24,38 @@ PACK = 4
 K_PASS = P * PACK
 PASSES = DIM // K_PASS
 CW = 512
-SSN = 128
-HEADS_PER_CHUNK = CW // D
+PER_CHUNK = CW // D
 TOK_TILES = TOK // P
-CHUNK_ORDER = (0, 3, 6, 1, 4, 7, 2, 5, 8)
+SSN = 64
+CHUNKS = (0, 3, 6, 1, 4, 7, 2, 5, 8)
+N_UNITS = len(CHUNKS) * PASSES
+N_PLANES = N_UNITS * PACK
+N_ITEMS = len(CHUNKS) * PER_CHUNK
+PLANES_PER_SLOT = 3
+G_COLS_HEAD = 192
+G_COLS_VALUE = 96
 
 
-def widen_on_vector(n, t):
-    if n < PASSES:
-        return t >= 2
-    return n % 5 == 4 and t == 3
+def quantise_slot(u):
+    return 4 + 4 * (u // PASSES) + u % PASSES
+
+
+def interleave_slot(u):
+    return quantise_slot(u - 2) + 1 if u >= 2 else 3 + u
+
+
+def widen_on_vector(n):
+    if n < 12:
+        return n % 2 == 1
+    return n % 8 == 7
+
+
+def is_head(i):
+    return 0 <= i < N_ITEMS and CHUNKS[i // PER_CHUNK] < 6
+
+
+def is_value(i):
+    return 0 <= i < N_ITEMS and CHUNKS[i // PER_CHUNK] >= 6
 
 
 def tile_fluxsingleattention_pa_kernel(
@@ -42,10 +64,11 @@ def tile_fluxsingleattention_pa_kernel(
     nc = tc.nc
     with ExitStack() as ctx:
         const = ctx.enter_context(tc.tile_pool(name="const", bufs=1))
-        wload = ctx.enter_context(tc.tile_pool(name="wload", bufs=len(CHUNK_ORDER) * PASSES))
+        wload = ctx.enter_context(tc.tile_pool(name="wload", bufs=N_UNITS))
         prep = ctx.enter_context(tc.tile_pool(name="prep", bufs=3))
-        epi = ctx.enter_context(tc.tile_pool(name="epi", bufs=3))
+        epi = ctx.enter_context(tc.tile_pool(name="epi", bufs=2))
         psum = ctx.enter_context(tc.psum_pool(name="psum", bufs=2))
+        ctx.enter_context(tc.manual_schedule())
 
         one_col = const.tile([P, SSN], F32, name="one_col")
         nc.vector.memset(one_col[:], 1.0)
@@ -58,98 +81,100 @@ def tile_fluxsingleattention_pa_kernel(
         swap = const.tile([P, P], F32, name="swap")
         ident_pairs = ident[:].rearrange("p (q j) -> p q j", j=2)
         swap_pairs = swap[:].rearrange("p (q j) -> p q j", j=2)
-        nc.vector.tensor_copy(out=swap_pairs[:, :, 0], in_=ident_pairs[:, :, 1])
-        nc.vector.tensor_copy(out=swap_pairs[:, :, 1], in_=ident_pairs[:, :, 0])
+        nc.gpsimd.tensor_copy(out=swap_pairs[:, :, 0], in_=ident_pairs[:, :, 1])
+        nc.gpsimd.tensor_copy(out=swap_pairs[:, :, 1], in_=ident_pairs[:, :, 0])
         stage = const.tile([P, P], BF16, name="stage")
         nc.vector.memset(stage[:], 0.0)
 
-        x_rows = hidden_states.flatten_outer_dims().rearrange("(i p) k -> i p k", p=P)
+        x_rows = hidden_states.flatten_outer_dims().rearrange("(i p) (g k) -> g p i k", p=P, k=K_PASS)
         w_rows = w_qkv_bytes.rearrange("(g p t) n -> g p t n", p=P, t=PACK)
-        units = [(c, g) for c in CHUNK_ORDER for g in range(PASSES)]
+        units = [(c, g) for c in CHUNKS for g in range(PASSES)]
 
         wscale = const.tile([P, PASSES, PACK], F32, name="wscale")
         nc.sync.dma_start(out=wscale[:], in_=w_qkv_scale.rearrange("(g p t) o -> p g (t o)", p=P, t=PACK))
 
         wbytes = {}
 
-        def load_unit(n):
-            c, g = units[n]
+        def load_unit(u):
+            c, g = units[u]
             wb = wload.tile([P, PACK, CW], U8, name="wbytes")
             nc.sync.dma_start(out=wb[:], in_=w_rows[g][:, :, c * CW : (c + 1) * CW])
-            wbytes[n] = wb
+            wbytes[u] = wb
 
         x_sb = []
-
-        def load_x(i):
-            xs = const.tile([P, DIM], BF16, name="x_sb%d" % i)
-            nc.sync.dma_start(out=xs[:], in_=x_rows[i])
+        for g in range(PASSES):
+            load_unit(g)
+            xs = const.tile([P, TOK_TILES, K_PASS], BF16, name="x_sb%d" % g)
+            nc.sync.dma_start(out=xs[:], in_=x_rows[g])
             x_sb.append(xs)
-
-        load_unit(0)
-        load_x(0)
-        load_x(1)
-        load_unit(1)
-        load_x(2)
-        load_x(3)
-        load_unit(2)
         nc.sync.dma_start(out=stage[0:36, :], in_=b_qkv.rearrange("(r d) -> r d", d=D))
         nc.sync.dma_start(out=stage[36:37, :], in_=norm_q_w.rearrange("(o d) -> o d", o=1))
         nc.sync.dma_start(out=stage[37:38, :], in_=norm_k_w.rearrange("(o d) -> o d", o=1))
         f_sb = const.tile([P, 2, 2 * D], BF16, name="f_sb")
         nc.sync.dma_start(out=f_sb[:], in_=image_rotary_emb.rearrange("o n (a s) q i j -> s (o n a) (q i j)", s=P))
-        for n in range(3, len(units)):
-            load_unit(n)
+        load_unit(3)
+        load_unit(4)
+        load_unit(5)
         bias_v = const.tile([P, DIM], BF16, name="bias_v")
         nc.sync.dma_start(out=bias_v[:], in_=b_qkv[2 * DIM : 3 * DIM].partition_broadcast(P))
+        for u in range(6, N_UNITS):
+            load_unit(u)
 
         x_codes = const.tile([P, PASSES, TOK], U32, name="x_codes", align_bytes=64)
         x_scl = const.tile([P, PASSES, TOK], U8, name="x_scl", align_bytes=64)
-        for g in range(PASSES):
+        x_grouped = []
+
+        def turn_x(g):
             xg = const.tile([P, TOK * PACK], BF16, name="xg%d" % g, align_bytes=64)
             xg_words = xg[:].bitcast(F32).rearrange("p (r u) -> p r u", u=2)
+            x_grouped.append(xg)
             for hf in range(2):
                 xt = psum.tile([P, 2, 2 * P], F32, name="acc", bufs=3)
                 for i2 in range(2):
-                    words = x_sb[2 * hf + i2][:].bitcast(F32)
+                    words = x_sb[g][:, 2 * hf + i2, :].bitcast(F32)
                     for u in range(2):
-                        nc.tensor.transpose(
-                            xt[:, u, i2 * P : (i2 + 1) * P], words[:, 256 * g + u : 256 * (g + 1) : 2], ident[:]
-                        )
+                        nc.tensor.transpose(xt[:, u, i2 * P : (i2 + 1) * P], words[:, u : 2 * P : 2], ident[:])
                 nc.vector.tensor_copy(
                     out=xg_words[:, 2 * P * hf : 2 * P * (hf + 1), :], in_=xt[:].rearrange("p u r -> p r u")
                 )
-            nc.vector.quantize_mx(out=x_codes[:, g, :].bitcast(FP8X4), scales=x_scl[:, g, :], in_=xg[:])
 
-        cols_ps = psum.tile([P, P], BF16, name="setup", bufs=1)
-        nc.tensor.transpose(cols_ps[:], stage[:], ident_bf[:])
+        def quantise_x(g):
+            nc.vector.quantize_mx(out=x_codes[:, g, :].bitcast(FP8X4), scales=x_scl[:, g, :], in_=x_grouped[g][:])
+
         cols = const.tile([P, 38], F32, name="cols")
-        nc.vector.tensor_copy(out=cols[:], in_=cols_ps[:, 0:38])
-
-        f4 = f_sb[:].rearrange("p a (q e) -> p a q e", e=4)
         f_same = const.tile([P, 2, D // 2, 2], F32, name="f_same")
         f_cross = const.tile([P, 2, D // 2, 2], F32, name="f_cross")
-        for j in range(2):
-            nc.vector.tensor_copy(out=f_same[:, :, :, j], in_=f4[:, :, :, 3 * j])
-            nc.vector.tensor_copy(out=f_cross[:, :, :, j], in_=f4[:, :, :, 2 - j])
-        g_ps = psum.tile([P, 4, P], F32, name="rot", bufs=2)
-        for kind, src in enumerate((f_same, f_cross)):
-            for a in range(2):
-                nc.tensor.transpose(g_ps[:, 2 * kind + a, :], src[:, a].rearrange("p q j -> p (q j)"), ident[:])
-        rope = []
-        for qk in range(2):
-            pair = []
+        rope = [[const.tile([P, TOK], F32, name="rope%d%d" % (qk, kind)) for kind in range(2)] for qk in range(2)]
+        rope_ps = []
+
+        def make_cols():
+            cols_ps = psum.tile([P, P], BF16, name="setup", bufs=1)
+            nc.tensor.transpose(cols_ps[:], stage[:], ident_bf[:])
+            nc.vector.tensor_copy(out=cols[:], in_=cols_ps[:, 0:38])
+
+        def pick_rope():
+            f4 = f_sb[:].rearrange("p a (q e) -> p a q e", e=4)
+            for j in range(2):
+                nc.gpsimd.tensor_copy(out=f_same[:, :, :, j], in_=f4[:, :, :, 3 * j])
+                nc.gpsimd.tensor_copy(out=f_cross[:, :, :, j], in_=f4[:, :, :, 2 - j])
+
+        def turn_rope():
+            g_ps = psum.tile([P, 4, P], F32, name="rot", bufs=2)
+            for kind, src in enumerate((f_same, f_cross)):
+                for a in range(2):
+                    nc.tensor.transpose(g_ps[:, 2 * kind + a, :], src[:, a].rearrange("p q j -> p (q j)"), ident[:])
+            rope_ps.append(g_ps)
+
+        def weigh_rope(qk):
             for kind in range(2):
-                gt = const.tile([P, TOK], F32, name="rope%d%d" % (qk, kind))
                 for b in range(B):
                     nc.vector.tensor_scalar(
-                        out=gt[:, b * S : (b + 1) * S],
-                        in0=g_ps[:, 2 * kind : 2 * kind + 2, :].rearrange("p a s -> p (a s)"),
+                        out=rope[qk][kind][:, b * S : (b + 1) * S],
+                        in0=rope_ps[0][:, 2 * kind : 2 * kind + 2, :].rearrange("p a s -> p (a s)"),
                         scalar1=cols[:, 36 + qk : 37 + qk],
                         scalar2=None,
                         op0=ALU.mult,
                     )
-                pair.append(gt)
-            rope.append(pair)
 
         planes = {}
         grouped = {}
@@ -157,118 +182,200 @@ def tile_fluxsingleattention_pa_kernel(
         w_scl = {}
 
         def widen(n):
-            c, g = units[n]
-            pl = prep.tile([P, PACK, CW], BF16, name="planes", bufs=6)
-            for t in range(PACK):
-                src = wbytes[n][:, t, :].bitcast(FP8)
-                if widen_on_vector(n, t):
-                    nc.vector.tensor_scalar(
-                        out=pl[:, t, :], in0=src, scalar1=wscale[:, g, t : t + 1], scalar2=None, op0=ALU.mult
-                    )
-                else:
-                    nc.scalar.activation(out=pl[:, t, :], in_=src, func=ACT.Copy, scale=wscale[:, g, t : t + 1])
-            planes[n] = pl
+            u, t = divmod(n, PACK)
+            g = units[u][1]
+            if t == 0:
+                pl = prep.tile([P, PACK, CW], BF16, name="planes", bufs=5)
+                planes[u] = pl
+            src = wbytes[u][:, t, :].bitcast(FP8)
+            if widen_on_vector(n):
+                nc.vector.tensor_scalar(
+                    out=planes[u][:, t, :], in0=src, scalar1=wscale[:, g, t : t + 1], scalar2=None, op0=ALU.mult
+                )
+            else:
+                nc.scalar.activation(out=planes[u][:, t, :], in_=src, func=ACT.Copy, scale=wscale[:, g, t : t + 1])
 
-        def interleave(n):
-            gr = prep.tile([P, CW, PACK], BF16, name="grouped", bufs=3, align_bytes=64)
-            nc.vector.tensor_copy(out=gr[:], in_=planes[n][:].rearrange("p t c -> p c t"))
-            grouped[n] = gr
+        def gpsimd_cols(u):
+            i = interleave_slot(u) - 9
+            if is_head(i):
+                return G_COLS_HEAD
+            if is_value(i):
+                return G_COLS_VALUE
+            return 0
 
-        def quantise(n):
-            c, g = units[n]
+        def interleave_gpsimd(u):
+            gr = prep.tile([P, CW, PACK], BF16, name="grouped", bufs=2, align_bytes=64)
+            grouped[u] = gr
+            gc = gpsimd_cols(u)
+            if gc > 0:
+                nc.gpsimd.tensor_scalar(
+                    out=gr[:, 0:gc, :],
+                    in0=planes[u][:, :, 0:gc].rearrange("p t c -> p c t"),
+                    scalar1=1.0,
+                    scalar2=0.0,
+                    op0=ALU.mult,
+                    op1=ALU.add,
+                )
+
+        def interleave_vector(u):
+            gc = gpsimd_cols(u)
+            nc.vector.tensor_copy(out=grouped[u][:, gc:CW, :], in_=planes[u][:, :, gc:CW].rearrange("p t c -> p c t"))
+
+        def quantise(u):
+            c, g = units[u]
             if g == 0:
-                wc = prep.tile([P, PASSES, CW], U32, name="w_codes", bufs=4, align_bytes=64)
-                ws = prep.tile([P, PASSES, CW], U8, name="w_scl", bufs=4, align_bytes=64)
+                wc = prep.tile([P, PASSES, CW], U32, name="w_codes", bufs=3, align_bytes=64)
+                ws = prep.tile([P, PASSES, CW], U8, name="w_scl", bufs=3, align_bytes=64)
                 w_codes[c] = wc
                 w_scl[c] = ws
             nc.vector.quantize_mx(
                 out=w_codes[c][:, g, :].bitcast(FP8X4),
                 scales=w_scl[c][:, g, :],
-                in_=grouped[n][:].rearrange("p c t -> p (c t)"),
+                in_=grouped[u][:].rearrange("p c t -> p (c t)"),
             )
 
-        def head(c, j):
-            qk = c // 3
-            h = (c % 3) * HEADS_PER_CHUNK + j
-            bcol = cols[:, qk * H + h : qk * H + h + 1]
-            dst = out_0 if qk == 0 else out_1
-            cs = slice(j * D, (j + 1) * D)
-            acc = psum.tile([P, TOK], F32, name="acc", bufs=3)
+        acc = {}
+        same = {}
+        cross = {}
+        sq = {}
+        rot = {}
+        ssq = {}
+        rms = {}
+        rstd = {}
+
+        def bias_col(i):
+            c, j = CHUNKS[i // PER_CHUNK], i % PER_CHUNK
+            r = c * PER_CHUNK + j
+            return cols[:, r : r + 1]
+
+        def multiply(i):
+            c, j = CHUNKS[i // PER_CHUNK], i % PER_CHUNK
+            js = slice(j * P, (j + 1) * P)
+            ac = psum.tile([P, TOK], F32, name="acc", bufs=3)
+            acc[i] = ac
             for g in range(PASSES):
-                nc.tensor.matmul_mx(
-                    out=acc[:],
-                    lhsT=w_codes[c][:, g, cs].bitcast(FP8X4),
-                    lhsT_scale=w_scl[c][:, g, cs],
-                    rhs=x_codes[:, g, :].bitcast(FP8X4),
-                    rhs_scale=x_scl[:, g, :],
-                    start=(g == 0),
-                    stop=(g == PASSES - 1),
-                )
-            same = epi.tile([P, TOK], F32, name="same")
-            cross = epi.tile([P, TOK], F32, name="cross")
-            sq = epi.tile([P, TOK], F32, name="sq")
+                if c < 6:
+                    nc.tensor.matmul_mx(
+                        out=ac[:],
+                        lhsT=w_codes[c][:, g, js].bitcast(FP8X4),
+                        lhsT_scale=w_scl[c][:, g, js],
+                        rhs=x_codes[:, g, :].bitcast(FP8X4),
+                        rhs_scale=x_scl[:, g, :],
+                        start=(g == 0),
+                        stop=(g == PASSES - 1),
+                    )
+                else:
+                    nc.tensor.matmul_mx(
+                        out=ac[:],
+                        lhsT=x_codes[:, g, js].bitcast(FP8X4),
+                        lhsT_scale=x_scl[:, g, js],
+                        rhs=w_codes[c][:, g, :].bitcast(FP8X4),
+                        rhs_scale=w_scl[c][:, g, :],
+                        start=(g == 0),
+                        stop=(g == PASSES - 1),
+                    )
+
+        def squares(i):
+            t = epi.tile([P, TOK], F32, name="sq")
+            sq[i] = t
+            nc.scalar.activation(out=t[:], in_=acc[i][:], func=ACT.Square, bias=bias_col(i), scale=1.0)
+
+        def sum_squares(i):
+            t = psum.tile([P, TOK_TILES, SSN], F32, name="ssq", bufs=2)
+            ssq[i] = t
+            for k in range(TOK_TILES):
+                nc.tensor.matmul(out=t[:, k, :], lhsT=sq[i][:, k * P : (k + 1) * P], rhs=one_col[:], start=True, stop=True)
+
+        def rope_terms(i):
+            qk = CHUNKS[i // PER_CHUNK] // 3
+            a = epi.tile([P, TOK], F32, name="same")
+            b = epi.tile([P, TOK], F32, name="cross")
+            same[i] = a
+            cross[i] = b
             nc.vector.scalar_tensor_tensor(
-                out=same[:], in0=acc[:], scalar=bcol, in1=rope[qk][0][:], op0=ALU.add, op1=ALU.mult
+                out=a[:], in0=acc[i][:], scalar=bias_col(i), in1=rope[qk][0][:], op0=ALU.add, op1=ALU.mult
             )
             nc.vector.scalar_tensor_tensor(
-                out=cross[:], in0=acc[:], scalar=bcol, in1=rope[qk][1][:], op0=ALU.add, op1=ALU.mult
+                out=b[:], in0=acc[i][:], scalar=bias_col(i), in1=rope[qk][1][:], op0=ALU.add, op1=ALU.mult
             )
-            nc.scalar.activation(out=sq[:], in_=acc[:], func=ACT.Square, bias=bcol, scale=1.0)
-            rot = psum.tile([P, TOK_TILES, D], F32, name="rot", bufs=2)
-            ssq = psum.tile([P, TOK_TILES, SSN], F32, name="ssq", bufs=2)
-            for i in range(TOK_TILES):
-                ts = slice(i * P, (i + 1) * P)
-                nc.tensor.matmul(out=rot[:, i, :], lhsT=same[:, ts], rhs=ident[:], is_transpose=True, start=True, stop=False)
-                nc.tensor.matmul(out=rot[:, i, :], lhsT=cross[:, ts], rhs=swap[:], is_transpose=True, start=False, stop=True)
-            for i in range(TOK_TILES):
-                ts = slice(i * P, (i + 1) * P)
-                nc.tensor.matmul(out=ssq[:, i, :], lhsT=sq[:, ts], rhs=one_col[:], start=True, stop=True)
-            rms = epi.tile([P, TOK_TILES], F32, name="rms")
-            rstd = epi.tile([P, TOK_TILES], F32, name="rstd")
-            nc.scalar.activation(out=rms[:], in_=ssq[:, :, 0], func=ACT.Sqrt, bias=EPS, scale=1.0 / D)
-            nc.vector.reciprocal(out=rstd[:], in_=rms[:])
-            res = epi.tile([P, TOK_TILES, D], F32, name="res", bufs=6)
-            for i in range(TOK_TILES):
-                nc.scalar.activation(out=res[:, i, :], in_=rot[:, i, :], func=ACT.Copy, scale=rstd[:, i : i + 1])
+
+        def turn_back(i):
+            t = psum.tile([P, TOK_TILES, D], F32, name="rot", bufs=2)
+            rot[i] = t
+            for k in range(TOK_TILES):
+                ks = slice(k * P, (k + 1) * P)
+                nc.tensor.matmul(out=t[:, k, :], lhsT=same[i][:, ks], rhs=ident[:], is_transpose=True, start=True, stop=False)
+                nc.tensor.matmul(out=t[:, k, :], lhsT=cross[i][:, ks], rhs=swap[:], is_transpose=True, start=False, stop=True)
+
+        def root(i):
+            t = epi.tile([P, TOK_TILES], F32, name="rms", bufs=3)
+            rms[i] = t
+            nc.scalar.activation(out=t[:], in_=ssq[i][:, :, 0], func=ACT.Sqrt, bias=EPS, scale=1.0 / D)
+
+        def invert(i):
+            t = epi.tile([P, TOK_TILES], F32, name="rstd", bufs=3)
+            rstd[i] = t
+            nc.vector.reciprocal(out=t[:], in_=rms[i][:])
+
+        def scale_out(i):
+            c, j = CHUNKS[i // PER_CHUNK], i % PER_CHUNK
+            h = (c % 3) * PER_CHUNK + j
+            dst = out_0 if c < 3 else out_1
+            res = epi.tile([P, TOK_TILES, D], F32, name="res", bufs=4)
+            for k in range(TOK_TILES):
+                nc.scalar.activation(out=res[:, k, :], in_=rot[i][:, k, :], func=ACT.Copy, scale=rstd[i][:, k : k + 1])
             for b in range(B):
                 nc.sync.dma_start(out=dst[b, h].rearrange("(a s) d -> s a d", s=P), in_=res[:, 2 * b : 2 * b + 2, :])
 
-        def value_tile(c, i):
-            h0 = (c - 6) * HEADS_PER_CHUNK
-            ts = slice(i * P, (i + 1) * P)
-            acc = psum.tile([P, CW], F32, name="acc", bufs=3)
-            for g in range(PASSES):
-                nc.tensor.matmul_mx(
-                    out=acc[:],
-                    lhsT=x_codes[:, g, ts].bitcast(FP8X4),
-                    lhsT_scale=x_scl[:, g, ts],
-                    rhs=w_codes[c][:, g, :].bitcast(FP8X4),
-                    rhs_scale=w_scl[c][:, g, :],
-                    start=(g == 0),
-                    stop=(g == PASSES - 1),
-                )
+        def add_bias(i):
+            c, k = CHUNKS[i // PER_CHUNK], i % PER_CHUNK
+            h0 = (c - 6) * PER_CHUNK
             val = epi.tile([P, CW], F32, name="val", bufs=4)
-            nc.vector.tensor_tensor(out=val[:], in0=acc[:], in1=bias_v[:, (c - 6) * CW : (c - 5) * CW], op=ALU.add)
-            b, a = divmod(i, 2)
+            nc.vector.tensor_tensor(out=val[:], in0=acc[i][:], in1=bias_v[:, (c - 6) * CW : (c - 5) * CW], op=ALU.add)
+            b, a = divmod(k, 2)
             nc.sync.dma_start(
-                out=out_2[b, h0 : h0 + HEADS_PER_CHUNK, a * P : (a + 1) * P, :].rearrange("h s d -> s h d"),
+                out=out_2[b, h0 : h0 + PER_CHUNK, a * P : (a + 1) * P, :].rearrange("h s d -> s h d"),
                 in_=val[:].rearrange("p (h d) -> p h d", d=D),
             )
 
-        def finish_chunk(c):
-            if c < 6:
-                for j in range(HEADS_PER_CHUNK):
-                    head(c, j)
-            else:
-                for i in range(TOK_TILES):
-                    value_tile(c, i)
-
-        for n in range(len(units) + 1):
-            if n < len(units):
+        for s in range(N_ITEMS + 11):
+            if is_head(s - 9):
+                root(s - 9)
+            if is_head(s - 10):
+                scale_out(s - 10)
+            if 0 <= s - 7 < N_ITEMS:
+                multiply(s - 7)
+            turn = [u for u in range(N_UNITS) if interleave_slot(u) == s]
+            for u in turn:
+                interleave_gpsimd(u)
+            if is_head(s - 9):
+                rope_terms(s - 9)
+                invert(s - 9)
+            if is_value(s - 9):
+                add_bias(s - 9)
+            if is_head(s - 8):
+                squares(s - 8)
+            if is_head(s - 9):
+                turn_back(s - 9)
+            if is_head(s - 8):
+                sum_squares(s - 8)
+            for n in range(PLANES_PER_SLOT * s, min(PLANES_PER_SLOT * (s + 1), N_PLANES)):
                 widen(n)
-                interleave(n)
-            if n >= 1:
-                quantise(n - 1)
-                c, g = units[n - 1]
-                if g == PASSES - 1:
-                    finish_chunk(c)
+            if s < PASSES:
+                turn_x(s)
+            if 1 <= s <= PASSES:
+                quantise_x(s - 1)
+            if s == 2:
+                pick_rope()
+            if s == 3:
+                make_cols()
+                turn_rope()
+            if s == 5:
+                weigh_rope(0)
+            if s == 6:
+                weigh_rope(1)
+            for u in turn:
+                interleave_vector(u)
+            for u in range(N_UNITS):
+                if quantise_slot(u) == s:
+                    quantise(u)

@@ -32,8 +32,8 @@ N_UNITS = len(CHUNKS) * PASSES
 N_PLANES = N_UNITS * PACK
 N_ITEMS = len(CHUNKS) * PER_CHUNK
 PLANES_PER_SLOT = 3
-G_COLS_HEAD = 192
-G_COLS_VALUE = 96
+G_COLS_HEAD = 112
+G_COLS_VALUE = 0
 
 
 def quantise_slot(u):
@@ -45,9 +45,7 @@ def interleave_slot(u):
 
 
 def widen_on_vector(n):
-    if n < 12:
-        return n % 2 == 1
-    return n % 8 == 7
+    return (n < 12 and n % 2 == 1) or n % 24 == 23
 
 
 def is_head(i):
@@ -73,7 +71,7 @@ def tile_fluxsingleattention_pa_kernel(
         one_col = const.tile([P, SSN], F32, name="one_col")
         nc.vector.memset(one_col[:], 1.0)
         warm = const.tile([P, 1], F32, name="warm")
-        nc.scalar.activation(out=warm[:], in_=one_col[:, 0:1], func=ACT.Sqrt)
+        nc.scalar.activation(out=warm[:], in_=one_col[:, 0:1], func=ACT.Abs_reciprocal_sqrt)
         ident = const.tile([P, P], F32, name="ident")
         make_identity(nc, ident[:])
         ident_bf = const.tile([P, P], BF16, name="ident_bf")
@@ -134,9 +132,14 @@ def tile_fluxsingleattention_pa_kernel(
                     words = x_sb[g][:, 2 * hf + i2, :].bitcast(F32)
                     for u in range(2):
                         nc.tensor.transpose(xt[:, u, i2 * P : (i2 + 1) * P], words[:, u : 2 * P : 2], ident[:])
-                nc.vector.tensor_copy(
-                    out=xg_words[:, 2 * P * hf : 2 * P * (hf + 1), :], in_=xt[:].rearrange("p u r -> p r u")
-                )
+                if hf == 0:
+                    nc.vector.tensor_copy(
+                        out=xg_words[:, 2 * P * hf : 2 * P * (hf + 1), :], in_=xt[:].rearrange("p u r -> p r u")
+                    )
+                else:
+                    nc.scalar.copy(
+                        out=xg_words[:, 2 * P * hf : 2 * P * (hf + 1), :], in_=xt[:].rearrange("p u r -> p r u")
+                    )
 
         def quantise_x(g):
             nc.vector.quantize_mx(out=x_codes[:, g, :].bitcast(FP8X4), scales=x_scl[:, g, :], in_=x_grouped[g][:])
@@ -240,7 +243,6 @@ def tile_fluxsingleattention_pa_kernel(
         sq = {}
         rot = {}
         ssq = {}
-        rms = {}
         rstd = {}
 
         def bias_col(i):
@@ -308,14 +310,9 @@ def tile_fluxsingleattention_pa_kernel(
                 nc.tensor.matmul(out=t[:, k, :], lhsT=cross[i][:, ks], rhs=swap[:], is_transpose=True, start=False, stop=True)
 
         def root(i):
-            t = epi.tile([P, TOK_TILES], F32, name="rms", bufs=3)
-            rms[i] = t
-            nc.scalar.activation(out=t[:], in_=ssq[i][:, :, 0], func=ACT.Sqrt, bias=EPS, scale=1.0 / D)
-
-        def invert(i):
             t = epi.tile([P, TOK_TILES], F32, name="rstd", bufs=3)
             rstd[i] = t
-            nc.vector.reciprocal(out=t[:], in_=rms[i][:])
+            nc.scalar.activation(out=t[:], in_=ssq[i][:, :, 0], func=ACT.Abs_reciprocal_sqrt, bias=EPS, scale=1.0 / D)
 
         def scale_out(i):
             c, j = CHUNKS[i // PER_CHUNK], i % PER_CHUNK
@@ -339,8 +336,6 @@ def tile_fluxsingleattention_pa_kernel(
             )
 
         for s in range(N_ITEMS + 11):
-            if is_head(s - 9):
-                root(s - 9)
             if is_head(s - 10):
                 scale_out(s - 10)
             if 0 <= s - 7 < N_ITEMS:
@@ -350,7 +345,6 @@ def tile_fluxsingleattention_pa_kernel(
                 interleave_gpsimd(u)
             if is_head(s - 9):
                 rope_terms(s - 9)
-                invert(s - 9)
             if is_value(s - 9):
                 add_bias(s - 9)
             if is_head(s - 8):
@@ -361,6 +355,10 @@ def tile_fluxsingleattention_pa_kernel(
                 sum_squares(s - 8)
             for n in range(PLANES_PER_SLOT * s, min(PLANES_PER_SLOT * (s + 1), N_PLANES)):
                 widen(n)
+                if n % PLANES_PER_SLOT == 1 and is_head(s - 9):
+                    root(s - 9)
+            if PLANES_PER_SLOT * s + 1 >= N_PLANES and is_head(s - 9):
+                root(s - 9)
             if s < PASSES:
                 turn_x(s)
             if 1 <= s <= PASSES:

@@ -27,7 +27,7 @@ CW = 512
 PER_CHUNK = CW // D
 TOK_TILES = TOK // P
 SSN = 64
-CHUNKS = (0, 3, 6, 1, 4, 7, 2, 5, 8)
+CHUNKS = (0, 3, 6, 1, 4, 2, 5, 7, 8)
 N_UNITS = len(CHUNKS) * PASSES
 N_PLANES = N_UNITS * PACK
 N_ITEMS = len(CHUNKS) * PER_CHUNK
@@ -44,16 +44,19 @@ def interleave_slot(u):
     return quantise_slot(u - 2) + 1 if u >= 2 else 3 + u
 
 
-def widen_on_vector(n):
-    return (n < 12 and n % 2 == 1) or n % 24 == 23
-
-
 def is_head(i):
     return 0 <= i < N_ITEMS and CHUNKS[i // PER_CHUNK] < 6
 
 
 def is_value(i):
     return 0 <= i < N_ITEMS and CHUNKS[i // PER_CHUNK] >= 6
+
+
+def widen_on_vector(n):
+    if n < 12:
+        return n % 2 == 1
+    s = n // PLANES_PER_SLOT
+    return n % PLANES_PER_SLOT == 2 and is_head(s - 9) and s % 4 < 3
 
 
 def tile_fluxsingleattention_pa_kernel(
@@ -99,23 +102,24 @@ def tile_fluxsingleattention_pa_kernel(
             nc.sync.dma_start(out=wb[:], in_=w_rows[g][:, :, c * CW : (c + 1) * CW])
             wbytes[u] = wb
 
-        x_sb = []
-        for g in range(PASSES):
-            load_unit(g)
-            xs = const.tile([P, TOK_TILES, K_PASS], BF16, name="x_sb%d" % g)
-            nc.sync.dma_start(out=xs[:], in_=x_rows[g])
-            x_sb.append(xs)
+        load_unit(0)
+        load_unit(1)
         nc.sync.dma_start(out=stage[0:36, :], in_=b_qkv.rearrange("(r d) -> r d", d=D))
         nc.sync.dma_start(out=stage[36:37, :], in_=norm_q_w.rearrange("(o d) -> o d", o=1))
         nc.sync.dma_start(out=stage[37:38, :], in_=norm_k_w.rearrange("(o d) -> o d", o=1))
         f_sb = const.tile([P, 2, 2 * D], BF16, name="f_sb")
         nc.sync.dma_start(out=f_sb[:], in_=image_rotary_emb.rearrange("o n (a s) q i j -> s (o n a) (q i j)", s=P))
-        load_unit(3)
-        load_unit(4)
-        load_unit(5)
+        x_sb = []
+        for g in range(PASSES):
+            load_unit(2 + g)
+            xs = const.tile([P, TOK_TILES, K_PASS], BF16, name="x_sb%d" % g)
+            nc.sync.dma_start(out=xs[:], in_=x_rows[g])
+            x_sb.append(xs)
+        for u in range(5, 9):
+            load_unit(u)
         bias_v = const.tile([P, DIM], BF16, name="bias_v")
         nc.sync.dma_start(out=bias_v[:], in_=b_qkv[2 * DIM : 3 * DIM].partition_broadcast(P))
-        for u in range(6, N_UNITS):
+        for u in range(9, N_UNITS):
             load_unit(u)
 
         x_codes = const.tile([P, PASSES, TOK], U32, name="x_codes", align_bytes=64)
@@ -171,12 +175,11 @@ def tile_fluxsingleattention_pa_kernel(
         def weigh_rope(qk):
             for kind in range(2):
                 for b in range(B):
-                    nc.vector.tensor_scalar(
+                    nc.scalar.activation(
                         out=rope[qk][kind][:, b * S : (b + 1) * S],
-                        in0=rope_ps[0][:, 2 * kind : 2 * kind + 2, :].rearrange("p a s -> p (a s)"),
-                        scalar1=cols[:, 36 + qk : 37 + qk],
-                        scalar2=None,
-                        op0=ALU.mult,
+                        in_=rope_ps[0][:, 2 * kind : 2 * kind + 2, :].rearrange("p a s -> p (a s)"),
+                        func=ACT.Copy,
+                        scale=cols[:, 36 + qk : 37 + qk],
                     )
 
         planes = {}
@@ -359,10 +362,10 @@ def tile_fluxsingleattention_pa_kernel(
                     root(s - 9)
             if PLANES_PER_SLOT * s + 1 >= N_PLANES and is_head(s - 9):
                 root(s - 9)
-            if s < PASSES:
-                turn_x(s)
-            if 1 <= s <= PASSES:
-                quantise_x(s - 1)
+            if 0 <= s - 3 < PASSES:
+                turn_x(s - 3)
+            if 1 <= s - 3 <= PASSES:
+                quantise_x(s - 4)
             if s == 2:
                 pick_rope()
             if s == 3:

@@ -31,17 +31,15 @@ CHUNKS = (0, 3, 6, 1, 4, 2, 5, 7, 8)
 N_UNITS = len(CHUNKS) * PASSES
 N_PLANES = N_UNITS * PACK
 N_ITEMS = len(CHUNKS) * PER_CHUNK
-PLANES_PER_SLOT = 3
-G_COLS_HEAD = 112
-G_COLS_VALUE = 0
-
-
-def quantise_slot(u):
-    return 4 + 4 * (u // PASSES) + u % PASSES
-
-
-def interleave_slot(u):
-    return quantise_slot(u - 2) + 1 if u >= 2 else 3 + u
+PAIRS = N_ITEMS // 2
+G_COLS_HEADS = 400
+G_COLS_VALUES = 192
+LAG_INTERLEAVE = 2
+LAG_MULTIPLY = 4
+LAG_SQUARES = 5
+LAG_WINDOW = 6
+LAG_SCALE = 7
+N_STEPS = PAIRS + LAG_SCALE + 1
 
 
 def is_head(i):
@@ -52,11 +50,22 @@ def is_value(i):
     return 0 <= i < N_ITEMS and CHUNKS[i // PER_CHUNK] >= 6
 
 
-def widen_on_vector(n):
-    if n < 12:
-        return n % 2 == 1
-    s = n // PLANES_PER_SLOT
-    return n % PLANES_PER_SLOT == 2 and is_head(s - 9) and s % 4 < 3
+def window_cols(j):
+    i = 2 * (j - LAG_WINDOW)
+    if is_head(i):
+        return G_COLS_HEADS
+    if is_value(i):
+        return G_COLS_VALUES
+    return 0
+
+
+def vector_planes(j):
+    if j < 2:
+        return 3
+    i = 2 * (j - LAG_WINDOW)
+    if is_head(i):
+        return 2
+    return 1
 
 
 def tile_fluxsingleattention_pa_kernel(
@@ -82,8 +91,10 @@ def tile_fluxsingleattention_pa_kernel(
         swap = const.tile([P, P], F32, name="swap")
         ident_pairs = ident[:].rearrange("p (q j) -> p q j", j=2)
         swap_pairs = swap[:].rearrange("p (q j) -> p q j", j=2)
-        nc.gpsimd.tensor_copy(out=swap_pairs[:, :, 0], in_=ident_pairs[:, :, 1])
-        nc.gpsimd.tensor_copy(out=swap_pairs[:, :, 1], in_=ident_pairs[:, :, 0])
+        for j in range(2):
+            nc.gpsimd.tensor_scalar(
+                out=swap_pairs[:, :, j], in0=ident_pairs[:, :, 1 - j], scalar1=1.0, scalar2=0.0, op0=ALU.mult, op1=ALU.add
+            )
         stage = const.tile([P, P], BF16, name="stage")
         nc.vector.memset(stage[:], 0.0)
 
@@ -104,22 +115,23 @@ def tile_fluxsingleattention_pa_kernel(
 
         load_unit(0)
         load_unit(1)
+        load_unit(2)
         nc.sync.dma_start(out=stage[0:36, :], in_=b_qkv.rearrange("(r d) -> r d", d=D))
         nc.sync.dma_start(out=stage[36:37, :], in_=norm_q_w.rearrange("(o d) -> o d", o=1))
         nc.sync.dma_start(out=stage[37:38, :], in_=norm_k_w.rearrange("(o d) -> o d", o=1))
         f_sb = const.tile([P, 2, 2 * D], BF16, name="f_sb")
         nc.sync.dma_start(out=f_sb[:], in_=image_rotary_emb.rearrange("o n (a s) q i j -> s (o n a) (q i j)", s=P))
+        load_unit(3)
         x_sb = []
         for g in range(PASSES):
-            load_unit(2 + g)
             xs = const.tile([P, TOK_TILES, K_PASS], BF16, name="x_sb%d" % g)
             nc.sync.dma_start(out=xs[:], in_=x_rows[g])
             x_sb.append(xs)
-        for u in range(5, 9):
-            load_unit(u)
+            load_unit(4 + 2 * g)
+            load_unit(5 + 2 * g)
         bias_v = const.tile([P, DIM], BF16, name="bias_v")
         nc.sync.dma_start(out=bias_v[:], in_=b_qkv[2 * DIM : 3 * DIM].partition_broadcast(P))
-        for u in range(9, N_UNITS):
+        for u in range(10, N_UNITS):
             load_unit(u)
 
         x_codes = const.tile([P, PASSES, TOK], U32, name="x_codes", align_bytes=64)
@@ -131,7 +143,7 @@ def tile_fluxsingleattention_pa_kernel(
             xg_words = xg[:].bitcast(F32).rearrange("p (r u) -> p r u", u=2)
             x_grouped.append(xg)
             for hf in range(2):
-                xt = psum.tile([P, 2, 2 * P], F32, name="acc", bufs=3)
+                xt = psum.tile([P, 2, 2 * P], F32, name="acc", bufs=4)
                 for i2 in range(2):
                     words = x_sb[g][:, 2 * hf + i2, :].bitcast(F32)
                     for u in range(2):
@@ -155,15 +167,17 @@ def tile_fluxsingleattention_pa_kernel(
         rope_ps = []
 
         def make_cols():
-            cols_ps = psum.tile([P, P], BF16, name="setup", bufs=1)
+            cols_ps = psum.tile([P, P], BF16, name="ssq", bufs=2)
             nc.tensor.transpose(cols_ps[:], stage[:], ident_bf[:])
             nc.vector.tensor_copy(out=cols[:], in_=cols_ps[:, 0:38])
 
         def pick_rope():
             f4 = f_sb[:].rearrange("p a (q e) -> p a q e", e=4)
             for j in range(2):
-                nc.gpsimd.tensor_copy(out=f_same[:, :, :, j], in_=f4[:, :, :, 3 * j])
-                nc.gpsimd.tensor_copy(out=f_cross[:, :, :, j], in_=f4[:, :, :, 2 - j])
+                for dst, e in ((f_same, 3 * j), (f_cross, 2 - j)):
+                    nc.gpsimd.tensor_scalar(
+                        out=dst[:, :, :, j], in0=f4[:, :, :, e], scalar1=1.0, scalar2=0.0, op0=ALU.mult, op1=ALU.add
+                    )
 
         def turn_rope():
             g_ps = psum.tile([P, 4, P], F32, name="rot", bufs=2)
@@ -187,32 +201,26 @@ def tile_fluxsingleattention_pa_kernel(
         w_codes = {}
         w_scl = {}
 
-        def widen(n):
+        def widen(n, on_vector):
             u, t = divmod(n, PACK)
             g = units[u][1]
             if t == 0:
-                pl = prep.tile([P, PACK, CW], BF16, name="planes", bufs=5)
+                pl = prep.tile([P, PACK, CW], BF16, name="planes", bufs=6)
                 planes[u] = pl
             src = wbytes[u][:, t, :].bitcast(FP8)
-            if widen_on_vector(n):
+            if on_vector:
                 nc.vector.tensor_scalar(
                     out=planes[u][:, t, :], in0=src, scalar1=wscale[:, g, t : t + 1], scalar2=None, op0=ALU.mult
                 )
             else:
                 nc.scalar.activation(out=planes[u][:, t, :], in_=src, func=ACT.Copy, scale=wscale[:, g, t : t + 1])
 
-        def gpsimd_cols(u):
-            i = interleave_slot(u) - 9
-            if is_head(i):
-                return G_COLS_HEAD
-            if is_value(i):
-                return G_COLS_VALUE
-            return 0
+        g_cols = {}
 
-        def interleave_gpsimd(u):
+        def interleave_gpsimd(u, gc):
+            g_cols[u] = gc
             gr = prep.tile([P, CW, PACK], BF16, name="grouped", bufs=2, align_bytes=64)
             grouped[u] = gr
-            gc = gpsimd_cols(u)
             if gc > 0:
                 nc.gpsimd.tensor_scalar(
                     out=gr[:, 0:gc, :],
@@ -224,7 +232,7 @@ def tile_fluxsingleattention_pa_kernel(
                 )
 
         def interleave_vector(u):
-            gc = gpsimd_cols(u)
+            gc = g_cols[u]
             nc.vector.tensor_copy(out=grouped[u][:, gc:CW, :], in_=planes[u][:, :, gc:CW].rearrange("p t c -> p c t"))
 
         def quantise(u):
@@ -256,7 +264,7 @@ def tile_fluxsingleattention_pa_kernel(
         def multiply(i):
             c, j = CHUNKS[i // PER_CHUNK], i % PER_CHUNK
             js = slice(j * P, (j + 1) * P)
-            ac = psum.tile([P, TOK], F32, name="acc", bufs=3)
+            ac = psum.tile([P, TOK], F32, name="acc", bufs=4)
             acc[i] = ac
             for g in range(PASSES):
                 if c < 6:
@@ -313,7 +321,7 @@ def tile_fluxsingleattention_pa_kernel(
                 nc.tensor.matmul(out=t[:, k, :], lhsT=cross[i][:, ks], rhs=swap[:], is_transpose=True, start=False, stop=True)
 
         def root(i):
-            t = epi.tile([P, TOK_TILES], F32, name="rstd", bufs=3)
+            t = epi.tile([P, TOK_TILES], F32, name="rstd", bufs=4)
             rstd[i] = t
             nc.scalar.activation(out=t[:], in_=ssq[i][:, :, 0], func=ACT.Abs_reciprocal_sqrt, bias=EPS, scale=1.0 / D)
 
@@ -330,7 +338,7 @@ def tile_fluxsingleattention_pa_kernel(
         def add_bias(i):
             c, k = CHUNKS[i // PER_CHUNK], i % PER_CHUNK
             h0 = (c - 6) * PER_CHUNK
-            val = epi.tile([P, CW], F32, name="val", bufs=4)
+            val = epi.tile([P, CW], F32, name="val", bufs=8)
             nc.vector.tensor_tensor(out=val[:], in0=acc[i][:], in1=bias_v[:, (c - 6) * CW : (c - 5) * CW], op=ALU.add)
             b, a = divmod(k, 2)
             nc.sync.dma_start(
@@ -338,45 +346,76 @@ def tile_fluxsingleattention_pa_kernel(
                 in_=val[:].rearrange("p (h d) -> p h d", d=D),
             )
 
-        for s in range(N_ITEMS + 11):
-            if is_head(s - 10):
-                scale_out(s - 10)
-            if 0 <= s - 7 < N_ITEMS:
-                multiply(s - 7)
-            turn = [u for u in range(N_UNITS) if interleave_slot(u) == s]
-            for u in turn:
-                interleave_gpsimd(u)
-            if is_head(s - 9):
-                rope_terms(s - 9)
-            if is_value(s - 9):
-                add_bias(s - 9)
-            if is_head(s - 8):
-                squares(s - 8)
-            if is_head(s - 9):
-                turn_back(s - 9)
-            if is_head(s - 8):
-                sum_squares(s - 8)
-            for n in range(PLANES_PER_SLOT * s, min(PLANES_PER_SLOT * (s + 1), N_PLANES)):
-                widen(n)
-                if n % PLANES_PER_SLOT == 1 and is_head(s - 9):
-                    root(s - 9)
-            if PLANES_PER_SLOT * s + 1 >= N_PLANES and is_head(s - 9):
-                root(s - 9)
-            if 0 <= s - 3 < PASSES:
-                turn_x(s - 3)
-            if 1 <= s - 3 <= PASSES:
-                quantise_x(s - 4)
-            if s == 2:
+        def pair(q):
+            return [i for i in (2 * q, 2 * q + 1) if 0 <= i < N_ITEMS]
+
+        next_plane = [0]
+
+        def widen_some(count, on_vector):
+            for k in range(count):
+                if next_plane[0] < N_PLANES:
+                    widen(next_plane[0], on_vector)
+                    next_plane[0] += 1
+
+        for j in range(N_STEPS):
+            chunk_pos, second = divmod(j - LAG_INTERLEAVE, 2)
+            preparing = 0 <= chunk_pos < len(CHUNKS)
+            ua, ub, uc = 3 * chunk_pos, 3 * chunk_pos + 1, 3 * chunk_pos + 2
+            nv = vector_planes(j)
+            ns = 6 - nv
+            if preparing:
+                interleave_gpsimd(ub if second else ua, window_cols(j))
+            for i in pair(j - LAG_WINDOW):
+                if is_head(i):
+                    rope_terms(i)
+                else:
+                    add_bias(i)
+            for i in pair(j - LAG_SCALE):
+                if is_head(i):
+                    scale_out(i)
+            for i in pair(j - LAG_WINDOW):
+                if is_head(i):
+                    root(i)
+            for i in pair(j - LAG_WINDOW):
+                if is_head(i):
+                    turn_back(i)
+            widen_some(ns // 2, False)
+            for i in pair(j - LAG_SQUARES):
+                if is_head(i):
+                    squares(i)
+            for i in pair(j - LAG_SQUARES):
+                if is_head(i):
+                    sum_squares(i)
+            widen_some(ns - ns // 2, False)
+            if j == 1:
                 pick_rope()
-            if s == 3:
+            if j == 2:
                 make_cols()
                 turn_rope()
-            if s == 5:
+            if j == 3:
                 weigh_rope(0)
-            if s == 6:
+            if j == 4:
                 weigh_rope(1)
-            for u in turn:
-                interleave_vector(u)
-            for u in range(N_UNITS):
-                if quantise_slot(u) == s:
-                    quantise(u)
+            if preparing:
+                interleave_vector(ub if second else ua)
+            widen_some(nv, True)
+            if not second:
+                if 0 <= chunk_pos - 1 < len(CHUNKS):
+                    quantise(uc - 3)
+                if preparing:
+                    quantise(ua)
+            elif preparing:
+                quantise(ub)
+                interleave_gpsimd(uc, 0)
+                interleave_vector(uc)
+            if j == 2:
+                turn_x(0)
+            if j == 3:
+                quantise_x(0)
+                turn_x(1)
+                turn_x(2)
+            if j == 4:
+                quantise_x(1)
+                quantise_x(2)
+            for i in pair(j - LAG_MULTIPLY):
+                multiply(i)

@@ -376,17 +376,15 @@ def tile_fluxsingleattention_pa_kernel(
             for i in pair(j - LAG_WINDOW):
                 if is_head(i):
                     root(i)
-            for i in pair(j - LAG_WINDOW):
-                if is_head(i):
-                    turn_back(i)
-            widen_some(ns // 2, False)
             for i in pair(j - LAG_SQUARES):
                 if is_head(i):
                     squares(i)
-            for i in pair(j - LAG_SQUARES):
-                if is_head(i):
-                    sum_squares(i)
-            widen_some(ns - ns // 2, False)
+            for e in range(2):
+                if is_head(2 * (j - LAG_WINDOW) + e):
+                    turn_back(2 * (j - LAG_WINDOW) + e)
+                if is_head(2 * (j - LAG_SQUARES) + e):
+                    sum_squares(2 * (j - LAG_SQUARES) + e)
+            widen_some(ns, False)
             if j == 1:
                 pick_rope()
             if j == 2:

@@ -233,7 +233,10 @@ def tile_fluxsingleattention_pa_kernel(
 
         def interleave_vector(u):
             gc = g_cols[u]
-            nc.vector.tensor_copy(out=grouped[u][:, gc:CW, :], in_=planes[u][:, :, gc:CW].rearrange("p t c -> p c t"))
+            nc.vector.tensor_copy(
+                out=grouped[u][:, gc:CW, :].rearrange("p (c i) t -> p c t i", i=4),
+                in_=planes[u][:, :, gc:CW].rearrange("p t (c i) -> p c t i", i=4),
+            )
 
         def quantise(u):
             c, g = units[u]

@@ -163,7 +163,7 @@ def tile_fluxsingleattention_pa_kernel(
         cols = const.tile([P, 38], F32, name="cols")
         f_same = const.tile([P, 2, D // 2, 2], F32, name="f_same")
         f_cross = const.tile([P, 2, D // 2, 2], F32, name="f_cross")
-        rope = [[const.tile([P, TOK], F32, name="rope%d%d" % (qk, kind)) for kind in range(2)] for qk in range(2)]
+        rope = [const.tile([P, 2, TOK], F32, name="rope%d" % qk) for qk in range(2)]
         rope_ps = []
 
         def make_cols():
@@ -187,14 +187,13 @@ def tile_fluxsingleattention_pa_kernel(
             rope_ps.append(g_ps)
 
         def weigh_rope(qk):
-            for kind in range(2):
-                for b in range(B):
-                    nc.scalar.activation(
-                        out=rope[qk][kind][:, b * S : (b + 1) * S],
-                        in_=rope_ps[0][:, 2 * kind : 2 * kind + 2, :].rearrange("p a s -> p (a s)"),
-                        func=ACT.Copy,
-                        scale=cols[:, 36 + qk : 37 + qk],
-                    )
+            for b in range(B):
+                nc.scalar.activation(
+                    out=rope[qk][:, :, b * S : (b + 1) * S],
+                    in_=rope_ps[0][:].rearrange("p (k a) s -> p k (a s)", k=2),
+                    func=ACT.Copy,
+                    scale=cols[:, 36 + qk : 37 + qk],
+                )
 
         planes = {}
         grouped = {}
@@ -292,7 +291,7 @@ def tile_fluxsingleattention_pa_kernel(
                     )
 
         def squares(i):
-            t = epi.tile([P, TOK], F32, name="sq")
+            t = epi.tile([P, TOK], F32, name="sq", bufs=4)
             sq[i] = t
             nc.scalar.activation(out=t[:], in_=acc[i][:], func=ACT.Square, bias=bias_col(i), scale=1.0)
 
@@ -304,15 +303,16 @@ def tile_fluxsingleattention_pa_kernel(
 
         def rope_terms(i):
             qk = CHUNKS[i // PER_CHUNK] // 3
-            a = epi.tile([P, TOK], F32, name="same")
-            b = epi.tile([P, TOK], F32, name="cross")
-            same[i] = a
-            cross[i] = b
+            both = epi.tile([P, 2, TOK], F32, name="terms", bufs=4)
+            same[i] = both[:, 0, :]
+            cross[i] = both[:, 1, :]
             nc.vector.scalar_tensor_tensor(
-                out=a[:], in0=acc[i][:], scalar=bias_col(i), in1=rope[qk][0][:], op0=ALU.add, op1=ALU.mult
-            )
-            nc.vector.scalar_tensor_tensor(
-                out=b[:], in0=acc[i][:], scalar=bias_col(i), in1=rope[qk][1][:], op0=ALU.add, op1=ALU.mult
+                out=both[:],
+                in0=acc[i][:].rearrange("p (o n) -> p o n", o=1).to_broadcast([P, 2, TOK]),
+                scalar=bias_col(i),
+                in1=rope[qk][:],
+                op0=ALU.add,
+                op1=ALU.mult,
             )
 
         def turn_back(i):
@@ -332,7 +332,7 @@ def tile_fluxsingleattention_pa_kernel(
             c, j = CHUNKS[i // PER_CHUNK], i % PER_CHUNK
             h = (c % 3) * PER_CHUNK + j
             dst = out_0 if c < 3 else out_1
-            res = epi.tile([P, TOK_TILES, D], F32, name="res", bufs=4)
+            res = epi.tile([P, TOK_TILES, D], F32, name="res", bufs=6)
             for k in range(TOK_TILES):
                 nc.scalar.activation(out=res[:, k, :], in_=rot[i][:, k, :], func=ACT.Copy, scale=rstd[i][:, k : k + 1])
             for b in range(B):

@@ -50,6 +50,10 @@ def is_value(i):
     return 0 <= i < N_ITEMS and CHUNKS[i // PER_CHUNK] >= 6
 
 
+def by_scalar_sum(i):
+    return i >= N_ITEMS - 10
+
+
 def window_cols(j):
     i = 2 * (j - LAG_WINDOW)
     if is_head(i):
@@ -296,6 +300,12 @@ def tile_fluxsingleattention_pa_kernel(
             nc.scalar.activation(out=t[:], in_=acc[i][:], func=ACT.Square, bias=bias_col(i), scale=1.0)
 
         def sum_squares(i):
+            if by_scalar_sum(i):
+                t = psum.tile([P, TOK_TILES, D], F32, name="ssq", bufs=2)
+                ssq[i] = t
+                for k in range(TOK_TILES):
+                    nc.tensor.transpose(t[:, k, :], sq[i][:, k * P : (k + 1) * P], ident[:])
+                return
             t = psum.tile([P, TOK_TILES, SSN], F32, name="ssq", bufs=2)
             ssq[i] = t
             for k in range(TOK_TILES):
@@ -326,6 +336,13 @@ def tile_fluxsingleattention_pa_kernel(
         def root(i):
             t = epi.tile([P, TOK_TILES], F32, name="rstd", bufs=4)
             rstd[i] = t
+            if by_scalar_sum(i):
+                sums = epi.tile([P, TOK_TILES], F32, name="sums", bufs=4)
+                for k in range(TOK_TILES):
+                    spent = epi.tile([P, D], F32, name="spent", bufs=2)
+                    nc.scalar.activation(out=spent[:], in_=ssq[i][:, k, :], func=ACT.Copy, accum_out=sums[:, k : k + 1])
+                nc.scalar.activation(out=t[:], in_=sums[:], func=ACT.Abs_reciprocal_sqrt, bias=EPS, scale=1.0 / D)
+                return
             nc.scalar.activation(out=t[:], in_=ssq[i][:, :, 0], func=ACT.Abs_reciprocal_sqrt, bias=EPS, scale=1.0 / D)
 
         def scale_out(i):

@@ -68,7 +68,7 @@ def vector_planes(j):
         return 3
     i = 2 * (j - LAG_WINDOW)
     if is_head(i):
-        return 2
+        return 2 + j % 2
     return 1
 
 

@@ -299,16 +299,18 @@ def tile_fluxsingleattention_pa_kernel(
             sq[i] = t
             nc.scalar.activation(out=t[:], in_=acc[i][:], func=ACT.Square, bias=bias_col(i), scale=1.0)
 
-        def sum_squares(i):
+        def sum_squares(i, tiles):
             if by_scalar_sum(i):
-                t = psum.tile([P, TOK_TILES, D], F32, name="ssq", bufs=2)
-                ssq[i] = t
-                for k in range(TOK_TILES):
-                    nc.tensor.transpose(t[:, k, :], sq[i][:, k * P : (k + 1) * P], ident[:])
+                if 0 in tiles:
+                    t = psum.tile([P, TOK_TILES, D], F32, name="ssq", bufs=2)
+                    ssq[i] = t
+                    for k in range(TOK_TILES):
+                        nc.tensor.transpose(t[:, k, :], sq[i][:, k * P : (k + 1) * P], ident[:])
                 return
-            t = psum.tile([P, TOK_TILES, SSN], F32, name="ssq", bufs=2)
-            ssq[i] = t
-            for k in range(TOK_TILES):
+            if 0 in tiles:
+                ssq[i] = psum.tile([P, TOK_TILES, SSN], F32, name="ssq", bufs=2)
+            t = ssq[i]
+            for k in tiles:
                 nc.tensor.matmul(out=t[:, k, :], lhsT=sq[i][:, k * P : (k + 1) * P], rhs=one_col[:], start=True, stop=True)
 
         def rope_terms(i):
@@ -393,17 +395,18 @@ def tile_fluxsingleattention_pa_kernel(
             for i in pair(j - LAG_SCALE):
                 if is_head(i):
                     scale_out(i)
-            for i in pair(j - LAG_WINDOW):
-                if is_head(i):
-                    root(i)
+            if is_head(2 * (j - LAG_WINDOW)):
+                root(2 * (j - LAG_WINDOW))
             for i in pair(j - LAG_SQUARES):
                 if is_head(i):
                     squares(i)
+            if is_head(2 * (j - LAG_WINDOW) + 1):
+                root(2 * (j - LAG_WINDOW) + 1)
             for e in range(2):
                 if is_head(2 * (j - LAG_WINDOW) + e):
                     turn_back(2 * (j - LAG_WINDOW) + e)
                 if is_head(2 * (j - LAG_SQUARES) + e):
-                    sum_squares(2 * (j - LAG_SQUARES) + e)
+                    sum_squares(2 * (j - LAG_SQUARES) + e, range(TOK_TILES) if e == 0 else range(TOK_TILES // 2))
             widen_some(ns, False)
             if j == 1:
                 pick_rope()
@@ -437,3 +440,5 @@ def tile_fluxsingleattention_pa_kernel(
                 quantise_x(2)
             for i in pair(j - LAG_MULTIPLY):
                 multiply(i)
+            if is_head(2 * (j - LAG_SQUARES) + 1):
+                sum_squares(2 * (j - LAG_SQUARES) + 1, range(TOK_TILES // 2, TOK_TILES))

from contextlib import ExitStack

import concourse.mybir as mybir
from concourse.masks import make_identity

B, S, H, D = 2, 256, 12, 128
DIM = H * D
TOK = B * S
EPS = 1e-6

FLOPS = 2 * TOK * DIM * 3 * DIM

F32 = mybir.dt.float32
BF16 = mybir.dt.bfloat16
U32 = mybir.dt.uint32
U8 = mybir.dt.uint8
FP8 = mybir.dt.float8_e4m3fn
FP8X4 = mybir.dt.float8_e4m3fn_x4
ACT = mybir.ActivationFunctionType
ALU = mybir.AluOpType

P = 128
PACK = 4
K_PASS = P * PACK
PASSES = DIM // K_PASS
CW = 512
PER_CHUNK = CW // D
TOK_TILES = TOK // P
SSN = 64
CHUNKS = (0, 3, 6, 1, 4, 2, 5, 7, 8)
N_UNITS = len(CHUNKS) * PASSES
N_PLANES = N_UNITS * PACK
N_ITEMS = len(CHUNKS) * PER_CHUNK
PAIRS = N_ITEMS // 2
G_COLS_HEADS = 400
G_COLS_VALUES = 192
LAG_INTERLEAVE = 2
LAG_MULTIPLY = 4
LAG_SQUARES = 5
LAG_WINDOW = 6
LAG_SCALE = 7
N_STEPS = PAIRS + LAG_SCALE + 1


def is_head(i):
    return 0 <= i < N_ITEMS and CHUNKS[i // PER_CHUNK] < 6


def is_value(i):
    return 0 <= i < N_ITEMS and CHUNKS[i // PER_CHUNK] >= 6


def by_scalar_sum(i):
    return i >= N_ITEMS - 10


def window_cols(j):
    i = 2 * (j - LAG_WINDOW)
    if is_head(i):
        return G_COLS_HEADS
    if is_value(i):
        return G_COLS_VALUES
    return 0


def vector_planes(j):
    if j < 2:
        return 3
    i = 2 * (j - LAG_WINDOW)
    if is_head(i):
        return 2 + j % 2
    return 1


def tile_fluxsingleattention_pa_kernel(
    tc, hidden_states, image_rotary_emb, w_qkv_bytes, w_qkv_scale, b_qkv, norm_q_w, norm_k_w, out_0, out_1, out_2
):
    nc = tc.nc
    with ExitStack() as ctx:
        const = ctx.enter_context(tc.tile_pool(name="const", bufs=1))
        wload = ctx.enter_context(tc.tile_pool(name="wload", bufs=N_UNITS))
        prep = ctx.enter_context(tc.tile_pool(name="prep", bufs=3))
        epi = ctx.enter_context(tc.tile_pool(name="epi", bufs=2))
        psum = ctx.enter_context(tc.psum_pool(name="psum", bufs=2))
        ctx.enter_context(tc.manual_schedule())

        one_col = const.tile([P, SSN], F32, name="one_col")
        nc.vector.memset(one_col[:], 1.0)
        warm = const.tile([P, 1], F32, name="warm")
        nc.scalar.activation(out=warm[:], in_=one_col[:, 0:1], func=ACT.Abs_reciprocal_sqrt)
        ident = const.tile([P, P], F32, name="ident")
        make_identity(nc, ident[:])
        ident_bf = const.tile([P, P], BF16, name="ident_bf")
        make_identity(nc, ident_bf[:])
        swap = const.tile([P, P], F32, name="swap")
        ident_pairs = ident[:].rearrange("p (q j) -> p q j", j=2)
        swap_pairs = swap[:].rearrange("p (q j) -> p q j", j=2)
        for j in range(2):
            nc.gpsimd.tensor_scalar(
                out=swap_pairs[:, :, j], in0=ident_pairs[:, :, 1 - j], scalar1=1.0, scalar2=0.0, op0=ALU.mult, op1=ALU.add
            )
        stage = const.tile([P, P], BF16, name="stage")
        nc.vector.memset(stage[:], 0.0)

        x_rows = hidden_states.flatten_outer_dims().rearrange("(i p) (g k) -> g p i k", p=P, k=K_PASS)
        w_rows = w_qkv_bytes.rearrange("(g p t) n -> g p t n", p=P, t=PACK)
        units = [(c, g) for c in CHUNKS for g in range(PASSES)]

        wscale = const.tile([P, PASSES, PACK], F32, name="wscale")
        nc.sync.dma_start(out=wscale[:], in_=w_qkv_scale.rearrange("(g p t) o -> p g (t o)", p=P, t=PACK))

        wbytes = {}

        def load_unit(u):
            c, g = units[u]
            wb = wload.tile([P, PACK, CW], U8, name="wbytes")
            nc.sync.dma_start(out=wb[:], in_=w_rows[g][:, :, c * CW : (c + 1) * CW])
            wbytes[u] = wb

        load_unit(0)
        load_unit(1)
        load_unit(2)
        nc.sync.dma_start(out=stage[0:36, :], in_=b_qkv.rearrange("(r d) -> r d", d=D))
        nc.sync.dma_start(out=stage[36:37, :], in_=norm_q_w.rearrange("(o d) -> o d", o=1))
        nc.sync.dma_start(out=stage[37:38, :], in_=norm_k_w.rearrange("(o d) -> o d", o=1))
        f_sb = const.tile([P, 2, 2 * D], BF16, name="f_sb")
        nc.sync.dma_start(out=f_sb[:], in_=image_rotary_emb.rearrange("o n (a s) q i j -> s (o n a) (q i j)", s=P))
        load_unit(3)
        x_sb = []
        for g in range(PASSES):
            xs = const.tile([P, TOK_TILES, K_PASS], BF16, name="x_sb%d" % g)
            nc.sync.dma_start(out=xs[:], in_=x_rows[g])
            x_sb.append(xs)
            load_unit(4 + 2 * g)
            load_unit(5 + 2 * g)
        bias_v = const.tile([P, DIM], BF16, name="bias_v")
        nc.sync.dma_start(out=bias_v[:], in_=b_qkv[2 * DIM : 3 * DIM].partition_broadcast(P))
        for u in range(10, N_UNITS):
            load_unit(u)

        x_codes = const.tile([P, PASSES, TOK], U32, name="x_codes", align_bytes=64)
        x_scl = const.tile([P, PASSES, TOK], U8, name="x_scl", align_bytes=64)
        x_grouped = []

        def turn_x(g):
            xg = const.tile([P, TOK * PACK], BF16, name="xg%d" % g, align_bytes=64)
            xg_words = xg[:].bitcast(F32).rearrange("p (r u) -> p r u", u=2)
            x_grouped.append(xg)
            for hf in range(2):
                xt = psum.tile([P, 2, 2 * P], F32, name="acc", bufs=4)
                for i2 in range(2):
                    words = x_sb[g][:, 2 * hf + i2, :].bitcast(F32)
                    for u in range(2):
                        nc.tensor.transpose(xt[:, u, i2 * P : (i2 + 1) * P], words[:, u : 2 * P : 2], ident[:])
                if hf == 0:
                    nc.vector.tensor_copy(
                        out=xg_words[:, 2 * P * hf : 2 * P * (hf + 1), :], in_=xt[:].rearrange("p u r -> p r u")
                    )
                else:
                    nc.scalar.copy(
                        out=xg_words[:, 2 * P * hf : 2 * P * (hf + 1), :], in_=xt[:].rearrange("p u r -> p r u")
                    )

        def quantise_x(g):
            nc.vector.quantize_mx(out=x_codes[:, g, :].bitcast(FP8X4), scales=x_scl[:, g, :], in_=x_grouped[g][:])

        cols = const.tile([P, 38], F32, name="cols")
        f_same = const.tile([P, 2, D // 2, 2], F32, name="f_same")
        f_cross = const.tile([P, 2, D // 2, 2], F32, name="f_cross")
        rope = [const.tile([P, 2, TOK], F32, name="rope%d" % qk) for qk in range(2)]
        rope_ps = []

        def make_cols():
            cols_ps = psum.tile([P, P], BF16, name="ssq", bufs=2)
            nc.tensor.transpose(cols_ps[:], stage[:], ident_bf[:])
            nc.vector.tensor_copy(out=cols[:], in_=cols_ps[:, 0:38])

        def pick_rope():
            f4 = f_sb[:].rearrange("p a (q e) -> p a q e", e=4)
            for j in range(2):
                for dst, e in ((f_same, 3 * j), (f_cross, 2 - j)):
                    nc.gpsimd.tensor_scalar(
                        out=dst[:, :, :, j], in0=f4[:, :, :, e], scalar1=1.0, scalar2=0.0, op0=ALU.mult, op1=ALU.add
                    )

        def turn_rope():
            g_ps = psum.tile([P, 4, P], F32, name="rot", bufs=2)
            for kind, src in enumerate((f_same, f_cross)):
                for a in range(2):
                    nc.tensor.transpose(g_ps[:, 2 * kind + a, :], src[:, a].rearrange("p q j -> p (q j)"), ident[:])
            rope_ps.append(g_ps)

        def weigh_rope(qk):
            for b in range(B):
                nc.scalar.activation(
                    out=rope[qk][:, :, b * S : (b + 1) * S],
                    in_=rope_ps[0][:].rearrange("p (k a) s -> p k (a s)", k=2),
                    func=ACT.Copy,
                    scale=cols[:, 36 + qk : 37 + qk],
                )

        planes = {}
        grouped = {}
        w_codes = {}
        w_scl = {}

        def widen(n, on_vector):
            u, t = divmod(n, PACK)
            g = units[u][1]
            if t == 0:
                pl = prep.tile([P, PACK, CW], BF16, name="planes", bufs=6)
                planes[u] = pl
            src = wbytes[u][:, t, :].bitcast(FP8)
            if on_vector:
                nc.vector.tensor_scalar(
                    out=planes[u][:, t, :], in0=src, scalar1=wscale[:, g, t : t + 1], scalar2=None, op0=ALU.mult
                )
            else:
                nc.scalar.activation(out=planes[u][:, t, :], in_=src, func=ACT.Copy, scale=wscale[:, g, t : t + 1])

        g_cols = {}

        def interleave_gpsimd(u, gc):
            g_cols[u] = gc
            gr = prep.tile([P, CW, PACK], BF16, name="grouped", bufs=2, align_bytes=64)
            grouped[u] = gr
            if gc > 0:
                nc.gpsimd.tensor_scalar(
                    out=gr[:, 0:gc, :],
                    in0=planes[u][:, :, 0:gc].rearrange("p t c -> p c t"),
                    scalar1=1.0,
                    scalar2=0.0,
                    op0=ALU.mult,
                    op1=ALU.add,
                )

        def interleave_vector(u):
            gc = g_cols[u]
            nc.vector.tensor_copy(
                out=grouped[u][:, gc:CW, :].rearrange("p (c i) t -> p c t i", i=4),
                in_=planes[u][:, :, gc:CW].rearrange("p t (c i) -> p c t i", i=4),
            )

        def quantise(u):
            c, g = units[u]
            if g == 0:
                wc = prep.tile([P, PASSES, CW], U32, name="w_codes", bufs=3, align_bytes=64)
                ws = prep.tile([P, PASSES, CW], U8, name="w_scl", bufs=3, align_bytes=64)
                w_codes[c] = wc
                w_scl[c] = ws
            nc.vector.quantize_mx(
                out=w_codes[c][:, g, :].bitcast(FP8X4),
                scales=w_scl[c][:, g, :],
                in_=grouped[u][:].rearrange("p c t -> p (c t)"),
            )

        acc = {}
        same = {}
        cross = {}
        sq = {}
        rot = {}
        ssq = {}
        rstd = {}

        def bias_col(i):
            c, j = CHUNKS[i // PER_CHUNK], i % PER_CHUNK
            r = c * PER_CHUNK + j
            return cols[:, r : r + 1]

        def multiply(i):
            c, j = CHUNKS[i // PER_CHUNK], i % PER_CHUNK
            js = slice(j * P, (j + 1) * P)
            ac = psum.tile([P, TOK], F32, name="acc", bufs=4)
            acc[i] = ac
            for g in range(PASSES):
                if c < 6:
                    nc.tensor.matmul_mx(
                        out=ac[:],
                        lhsT=w_codes[c][:, g, js].bitcast(FP8X4),
                        lhsT_scale=w_scl[c][:, g, js],
                        rhs=x_codes[:, g, :].bitcast(FP8X4),
                        rhs_scale=x_scl[:, g, :],
                        start=(g == 0),
                        stop=(g == PASSES - 1),
                    )
                else:
                    nc.tensor.matmul_mx(
                        out=ac[:],
                        lhsT=x_codes[:, g, js].bitcast(FP8X4),
                        lhsT_scale=x_scl[:, g, js],
                        rhs=w_codes[c][:, g, :].bitcast(FP8X4),
                        rhs_scale=w_scl[c][:, g, :],
                        start=(g == 0),
                        stop=(g == PASSES - 1),
                    )

        def squares(i):
            t = epi.tile([P, TOK], F32, name="sq", bufs=4)
            sq[i] = t
            nc.scalar.activation(out=t[:], in_=acc[i][:], func=ACT.Square, bias=bias_col(i), scale=1.0)

        def sum_squares(i, tiles):
            if by_scalar_sum(i):
                if 0 in tiles:
                    t = psum.tile([P, TOK_TILES, D], F32, name="ssq", bufs=2)
                    ssq[i] = t
                    for k in range(TOK_TILES):
                        nc.tensor.transpose(t[:, k, :], sq[i][:, k * P : (k + 1) * P], ident[:])
                return
            if 0 in tiles:
                ssq[i] = psum.tile([P, TOK_TILES, SSN], F32, name="ssq", bufs=2)
            t = ssq[i]
            for k in tiles:
                nc.tensor.matmul(out=t[:, k, :], lhsT=sq[i][:, k * P : (k + 1) * P], rhs=one_col[:], start=True, stop=True)

        def rope_terms(i):
            qk = CHUNKS[i // PER_CHUNK] // 3
            both = epi.tile([P, 2, TOK], F32, name="terms", bufs=4)
            same[i] = both[:, 0, :]
            cross[i] = both[:, 1, :]
            nc.vector.scalar_tensor_tensor(
                out=both[:],
                in0=acc[i][:].rearrange("p (o n) -> p o n", o=1).to_broadcast([P, 2, TOK]),
                scalar=bias_col(i),
                in1=rope[qk][:],
                op0=ALU.add,
                op1=ALU.mult,
            )

        def turn_back(i):
            t = psum.tile([P, TOK_TILES, D], F32, name="rot", bufs=2)
            rot[i] = t
            for k in range(TOK_TILES):
                ks = slice(k * P, (k + 1) * P)
                nc.tensor.matmul(out=t[:, k, :], lhsT=same[i][:, ks], rhs=ident[:], is_transpose=True, start=True, stop=False)
                nc.tensor.matmul(out=t[:, k, :], lhsT=cross[i][:, ks], rhs=swap[:], is_transpose=True, start=False, stop=True)

        def root(i):
            t = epi.tile([P, TOK_TILES], F32, name="rstd", bufs=4)
            rstd[i] = t
            if by_scalar_sum(i):
                sums = epi.tile([P, TOK_TILES], F32, name="sums", bufs=4)
                for k in range(TOK_TILES):
                    spent = epi.tile([P, D], F32, name="spent", bufs=2)
                    nc.scalar.activation(out=spent[:], in_=ssq[i][:, k, :], func=ACT.Copy, accum_out=sums[:, k : k + 1])
                nc.scalar.activation(out=t[:], in_=sums[:], func=ACT.Abs_reciprocal_sqrt, bias=EPS, scale=1.0 / D)
                return
            nc.scalar.activation(out=t[:], in_=ssq[i][:, :, 0], func=ACT.Abs_reciprocal_sqrt, bias=EPS, scale=1.0 / D)

        def scale_out(i):
            c, j = CHUNKS[i // PER_CHUNK], i % PER_CHUNK
            h = (c % 3) * PER_CHUNK + j
            dst = out_0 if c < 3 else out_1
            res = epi.tile([P, TOK_TILES, D], F32, name="res", bufs=6)
            for k in range(TOK_TILES):
                nc.scalar.activation(out=res[:, k, :], in_=rot[i][:, k, :], func=ACT.Copy, scale=rstd[i][:, k : k + 1])
            for b in range(B):
                nc.sync.dma_start(out=dst[b, h].rearrange("(a s) d -> s a d", s=P), in_=res[:, 2 * b : 2 * b + 2, :])

        def add_bias(i):
            c, k = CHUNKS[i // PER_CHUNK], i % PER_CHUNK
            h0 = (c - 6) * PER_CHUNK
            val = epi.tile([P, CW], F32, name="val", bufs=8)
            nc.vector.tensor_tensor(out=val[:], in0=acc[i][:], in1=bias_v[:, (c - 6) * CW : (c - 5) * CW], op=ALU.add)
            b, a = divmod(k, 2)
            nc.sync.dma_start(
                out=out_2[b, h0 : h0 + PER_CHUNK, a * P : (a + 1) * P, :].rearrange("h s d -> s h d"),
                in_=val[:].rearrange("p (h d) -> p h d", d=D),
            )

        def pair(q):
            return [i for i in (2 * q, 2 * q + 1) if 0 <= i < N_ITEMS]

        next_plane = [0]

        def widen_some(count, on_vector):
            for k in range(count):
                if next_plane[0] < N_PLANES:
                    widen(next_plane[0], on_vector)
                    next_plane[0] += 1

        for j in range(N_STEPS):
            chunk_pos, second = divmod(j - LAG_INTERLEAVE, 2)
            preparing = 0 <= chunk_pos < len(CHUNKS)
            ua, ub, uc = 3 * chunk_pos, 3 * chunk_pos + 1, 3 * chunk_pos + 2
            nv = vector_planes(j)
            ns = 6 - nv
            if preparing:
                interleave_gpsimd(ub if second else ua, window_cols(j))
            for i in pair(j - LAG_WINDOW):
                if is_head(i):
                    rope_terms(i)
                else:
                    add_bias(i)
            for i in pair(j - LAG_SCALE):
                if is_head(i):
                    scale_out(i)
            if is_head(2 * (j - LAG_WINDOW)):
                root(2 * (j - LAG_WINDOW))
            for i in pair(j - LAG_SQUARES):
                if is_head(i):
                    squares(i)
            if is_head(2 * (j - LAG_WINDOW) + 1):
                root(2 * (j - LAG_WINDOW) + 1)
            for e in range(2):
                if is_head(2 * (j - LAG_WINDOW) + e):
                    turn_back(2 * (j - LAG_WINDOW) + e)
                if is_head(2 * (j - LAG_SQUARES) + e):
                    sum_squares(2 * (j - LAG_SQUARES) + e, range(TOK_TILES) if e == 0 else range(TOK_TILES // 2))
            widen_some(ns, False)
            if j == 1:
                pick_rope()
            if j == 2:
                make_cols()
                turn_rope()
            if j == 3:
                weigh_rope(0)
            if j == 4:
                weigh_rope(1)
            if preparing:
                interleave_vector(ub if second else ua)
            widen_some(nv, True)
            if not second:
                if 0 <= chunk_pos - 1 < len(CHUNKS):
                    quantise(uc - 3)
                if preparing:
                    quantise(ua)
            elif preparing:
                quantise(ub)
                interleave_gpsimd(uc, 0)
                interleave_vector(uc)
            if j == 2:
                turn_x(0)
            if j == 3:
                quantise_x(0)
                turn_x(1)
                turn_x(2)
            if j == 4:
                quantise_x(1)
                quantise_x(2)
            for i in pair(j - LAG_MULTIPLY):
                multiply(i)
            if is_head(2 * (j - LAG_SQUARES) + 1):
                sum_squares(2 * (j - LAG_SQUARES) + 1, range(TOK_TILES // 2, TOK_TILES))
